import numpy as np
import ml_dtypes


def mxq(x, axis, fmt="e4m3"):
    dtype, down = {"e4m3": (ml_dtypes.float8_e4m3fn, 7), "e5m2": (ml_dtypes.float8_e5m2, 14)}[fmt]
    v = np.moveaxis(np.asarray(x, np.float32).astype(ml_dtypes.bfloat16).astype(np.float64), axis, -1)
    blocks = v.reshape(v.shape[:-1] + (-1, 32))
    amax = np.abs(blocks).max(-1, keepdims=True)
    byte = np.maximum(np.where(amax > 0, np.frexp(amax)[1] - 1 + 127, 0) - down, 1)
    scale = np.exp2(byte - 127.0)
    codes = (blocks / scale).astype(np.float32).astype(dtype).astype(np.float64)
    return np.moveaxis((codes * scale).reshape(v.shape), -1, axis)


WIDE = False


def mx_kscale(k):
    if not WIDE:
        return np.ones(k)
    levels = np.array([10, -10, 5, -5, 0])
    if k % 512:
        return np.exp2(np.random.permutation(np.resize(levels, k // 32))).repeat(32)
    a = np.empty((k // 512, 16))
    for p in range(k // 512):
        a[p, :8] = np.random.permutation(np.resize(levels, 8))
        for g in range(8):
            far = levels[np.abs(levels - a[p, g]) >= 10]
            a[p, g + 8] = far[np.random.randint(len(far))]
    return np.exp2(a.ravel()).repeat(32)


BF16 = ml_dtypes.bfloat16


def bf(x):
    return np.asarray(x, np.float32).astype(BF16)


def f64(x):
    return np.asarray(x).astype(np.float64)


E2M1 = np.array([0.0, 0.5, 1.0, 1.5, 2.0, 3.0, 4.0, 6.0, -0.0, -0.5, -1.0, -1.5, -2.0, -3.0, -4.0, -6.0])


def pack_weight(w, fmt):
    k, n = w.shape
    w = f64(bf(w)).reshape(k // 32, 32, n)
    amax = np.abs(w).max(1)
    if fmt == "e4m3":
        byte = np.frexp(amax)[1] - 1 + 127 - 7
    else:
        mant, ex = np.frexp(amax / 6.0)
        byte = np.where(mant > 0.5, ex, ex - 1) + 127
    byte = np.clip(np.where(amax > 0, byte, 1), 1, 254)
    scaled = (w * np.exp2(127.0 - byte)[:, None, :]).reshape(k, n).astype(np.float32)
    by_word = np.ascontiguousarray(scaled.reshape(k // 512, 128, 4, n).transpose(0, 1, 3, 2))
    if fmt == "e4m3":
        words = by_word.astype(ml_dtypes.float8_e4m3fn).view(np.uint8)
    else:
        c = by_word.astype(ml_dtypes.float4_e2m1fn).view(np.uint8) & 0xF
        words = c[..., 0::2] | (c[..., 1::2] << 4)
    return np.ascontiguousarray(words), np.ascontiguousarray(byte.astype(np.uint8).reshape(k // 512, 16, n))


def unpack_weight(words, scales, fmt):
    g, p, n, _ = words.shape
    if fmt == "e4m3":
        vals = np.ascontiguousarray(words).view(ml_dtypes.float8_e4m3fn).astype(np.float64)
    else:
        nib = np.empty((g, p, n, 4), np.uint8)
        nib[..., 0::2] = words & 0xF
        nib[..., 1::2] = words >> 4
        vals = E2M1[nib]
    vals = vals * np.repeat(np.exp2(scales.astype(np.float64) - 127.0), 8, axis=1)[..., None]
    return vals.transpose(0, 1, 3, 2).reshape(g * 512, n)


B, L, H, T, HEADS = 1, 128, 2048, 3, 32
DH = H // HEADS
FMT = "e4m3"


def rope_tables(seq_len, dim):
    inv_freq = 1.0 / (10000.0 ** (np.arange(0, dim, 2, dtype=np.float64) / dim))
    ang = np.arange(seq_len, dtype=np.float64)[:, None] * inv_freq[None, :]
    return np.sin(ang), np.cos(ang)


def apply_rotary(x, sin, cos):
    s = sin[None, :, None, None, :]
    c = cos[None, :, None, None, :]
    x1, x2 = x[..., 0::2], x[..., 1::2]
    return np.concatenate([x1 * c - x2 * s, x2 * c + x1 * s], axis=-1)


def draw0():
    s = mx_kscale(H)
    u = np.tile(np.repeat(mx_kscale(H).reshape(HEADS, DH)[:, : DH // 2], 2, axis=1).reshape(H), T)
    a = 0.5 / np.sqrt(DH)
    hidden_state = bf(np.random.standard_normal((B, L, H)) * s)
    Wq_words, Wq_scales = pack_weight(np.random.standard_normal((H, H * T)) * a / s[:, None] * u, FMT)
    bq = bf(np.random.standard_normal(H * T) * 0.3 * u)
    Wk_words, Wk_scales = pack_weight(np.random.standard_normal((H, H * T)) * a / s[:, None] / u, FMT)
    bk = bf(np.random.standard_normal(H * T) * 0.3 / u)
    return {
        "hidden_state": hidden_state,
        "Wq_words": Wq_words,
        "Wq_scales": Wq_scales,
        "bq": bq,
        "Wk_words": Wk_words,
        "Wk_scales": Wk_scales,
        "bk": bk,
    }


def core(hidden_state, Wq_words, Wq_scales, bq, Wk_words, Wk_scales, bk):
    scale = (H // 12) ** (-0.5)
    sin, cos = rope_tables(L, DH)
    xq = mxq(f64(hidden_state), 2, "e4m3")
    q = ((xq @ unpack_weight(Wq_words, Wq_scales, FMT)) + f64(bq)).reshape(B, L, T, HEADS, DH)
    k = ((xq @ unpack_weight(Wk_words, Wk_scales, FMT)) + f64(bk)).reshape(B, L, T, HEADS, DH)
    q = apply_rotary(q, sin, cos).reshape(B, L, T, H)
    k = apply_rotary(k, sin, cos).reshape(B, L, T, H)
    qq = mxq(q, 3, "e4m3")
    kq = mxq(k, 3, "e4m3")
    score = (qq.transpose(0, 2, 1, 3) @ kq.transpose(0, 2, 3, 1)).transpose(0, 2, 3, 1) * (scale / HEADS)
    return score


def e4m3fn_bytes(y):
    return np.clip(np.asarray(y, np.float64), -448.0, 448.0).astype(np.float32).astype(ml_dtypes.float8_e4m3fn).view(np.uint8)


def e4m3fn_values(b):
    return np.asarray(b, np.uint8).view(ml_dtypes.float8_e4m3fn).astype(np.float64)


def setup_inputs():
    d = draw0()
    x0 = np.asarray(d['hidden_state']).astype(np.float64)
    s = (np.max(np.abs(x0), axis=(0, 1), keepdims=True) / 448.0).astype(np.float32)
    out = {}
    for k, v in d.items():
        if k == 'hidden_state':
            out['hidden_state_bytes'] = e4m3fn_bytes(x0 / s.astype(np.float64))
            out['hidden_state_scale'] = s
        else:
            out[k] = v
    return out


def reference(hidden_state_bytes, hidden_state_scale, Wq_words, Wq_scales, bq, Wk_words, Wk_scales, bk):
    return core(e4m3fn_values(hidden_state_bytes) * hidden_state_scale.astype(np.float64), Wq_words, Wq_scales, bq, Wk_words, Wk_scales, bk)

@@ -1,0 +1,375 @@
+import math
+from contextlib import ExitStack
+
+import concourse.mybir as mybir
+from concourse.masks import make_identity
+
+F32 = mybir.dt.float32
+BF16 = mybir.dt.bfloat16
+U32 = mybir.dt.uint32
+I32 = mybir.dt.int32
+U8 = mybir.dt.uint8
+FP8 = mybir.dt.float8_e4m3fn
+FP8X4 = mybir.dt.float8_e4m3fn_x4
+ALU = mybir.AluOpType
+ACT = mybir.ActivationFunctionType
+
+P = 128
+HID = 2048
+TAGS = 3
+HEADS = 32
+DH = 64
+M = DH // 2
+GROUPS = HID // 512
+NOUT = HID * TAGS
+BANK = 512
+UNIT = 1024
+UNITS = 2 * NOUT // UNIT
+HG = 8
+SCORE_SCALE = (HID // 12) ** (-0.5) / HEADS
+FLOPS = 2 * P * HID * 2 * NOUT + 2 * TAGS * P * P * HID
+
+VEC_M = 20
+W_BUFS = 18
+AHEAD = 14
+
+
+def tile_ner_w_w8_kernel(
+    tc, x_bytes, x_scale, wq_words, wq_scales, bq, wk_words, wk_scales, bk, out
+):
+    nc = tc.nc
+    words = (wq_words, wk_words)
+    wscales = (wq_scales, wk_scales)
+
+    with ExitStack() as ctx:
+        keep = ctx.enter_context(tc.tile_pool(name="keep", bufs=1))
+        wpool = ctx.enter_context(tc.tile_pool(name="weights", bufs=W_BUFS))
+        work = ctx.enter_context(tc.tile_pool(name="work", bufs=2))
+        acc_pool = ctx.enter_context(tc.psum_pool(name="acc", bufs=4))
+        tr_pool = ctx.enter_context(tc.psum_pool(name="tr", bufs=2))
+        bc_pool = ctx.enter_context(tc.psum_pool(name="bc", bufs=1))
+        sc_pool = ctx.enter_context(tc.psum_pool(name="sc", bufs=1))
+        ctx.enter_context(tc.manual_schedule())
+
+        xb = keep.tile([P, HID], U8, name="xb", align_bytes=64)
+        xs = keep.tile([P, GROUPS, 4], F32, name="xs", align_bytes=64)
+        brow = keep.tile([P, 1536], BF16, name="brow", align_bytes=64)
+        packed_q = keep.tile([P, NOUT], U8, name="packed_q", align_bytes=64)
+        packed_k = keep.tile([P, NOUT], U8, name="packed_k", align_bytes=64)
+        packed = (packed_q, packed_k)
+
+        nc.gpsimd.memset(brow[:].bitcast(U32), 0)
+        nc.vector.memset(packed_q[:].bitcast(I32), 0)
+        pos = keep.tile([P, 1], F32, name="pos", align_bytes=64)
+        nc.gpsimd.iota(pos[:], [[0, 1]], base=0, channel_multiplier=1, allow_small_or_imprecise_dtypes=True)
+        ident = keep.tile([P, P], F32, name="ident", align_bytes=64)
+        make_identity(nc, ident[:])
+        ident_b = keep.tile([P, P], BF16, name="ident_b", align_bytes=64)
+        make_identity(nc, ident_b[:])
+        nc.gpsimd.memset(packed_k[:].bitcast(I32), 0)
+
+        nc.sync.dma_start(out=xb[:], in_=x_bytes.rearrange("b l h -> (b l) h"))
+        nc.sync.dma_start(out=xs[:], in_=x_scale.rearrange("a b (g p t) -> p (a b g) t", p=P, t=4))
+        nc.sync.dma_start(out=brow[0:4, :], in_=bq.rearrange("(r n) -> r n", r=4))
+        nc.sync.dma_start(out=brow[4:8, :], in_=bk.rearrange("(r n) -> r n", r=4))
+
+        def load_scales(z):
+            for quad in range(4):
+                nc.sync.dma_start(
+                    out=packed[z][32 * quad : 32 * quad + 16, :].bitcast(I32),
+                    in_=wscales[z][:, 4 * quad : 4 * quad + 4, :].bitcast(I32),
+                )
+
+        plan = []
+        for half in range(2):
+            for g in (0, 2):
+                plan.append((0, 1024 * half, 1024, g, 2))
+        for c in range(1, 4):
+            for g in range(GROUPS):
+                plan.append((c, 0, 2048, g, 1))
+        for c in (4, 5):
+            for half in range(2):
+                if c == 5 and half == 1:
+                    break
+                for g in (0, 2):
+                    plan.append((c, 1024 * half, 1024, g, 2))
+        plan.append((5, 1024, 512, 0, 2))
+        plan.append((5, 1024, 512, 2, 2))
+        plan.append((5, 1536, 256, 0, 4))
+        plan.append((5, 1792, 256, 0, 4))
+        loaded = {}
+        count = [0]
+
+        def load_until(n):
+            while count[0] < min(n, len(plan)):
+                c, c0, width, g, ng = plan[count[0]]
+                if count[0] == 0:
+                    load_scales(0)
+                if count[0] == 4:
+                    load_scales(1)
+                z = c % 2
+                col = (c // 2) * HID + c0
+                w = wpool.tile([P, ng, width], U32, name="w", tag="w", align_bytes=64)
+                nc.sync.dma_start(
+                    out=w[:].bitcast(I32),
+                    in_=words[z].rearrange("g p n t -> p g (n t)")[:, g : g + ng, 4 * col : 4 * (col + width)].bitcast(I32),
+                )
+                for k in range(ng):
+                    loaded[(c, c0, g + k)] = (w, k, width)
+                count[0] += 1
+
+        load_until(AHEAD)
+
+        turns = keep.tile([P, M], F32, name="turns", align_bytes=64)
+        for m in range(8):
+            nc.vector.tensor_scalar(
+                out=turns[:, m : m + 1], in0=pos[:], scalar1=10000.0 ** (-m / M) / (2.0 * math.pi), scalar2=None, op0=ALU.mult
+            )
+        nc.vector.tensor_scalar(out=turns[:, 8:16], in0=turns[:, 0:8], scalar1=0.1, scalar2=None, op0=ALU.mult)
+        nc.vector.tensor_scalar(out=turns[:, 16:32], in0=turns[:, 0:16], scalar1=0.01, scalar2=None, op0=ALU.mult)
+        turns_i = keep.tile([P, M], I32, name="turns_i", align_bytes=64)
+        turns_f = keep.tile([P, M], F32, name="turns_f", align_bytes=64)
+        angle = keep.tile([P, 2 * M], F32, name="angle", align_bytes=64)
+        angle_w = keep.tile([P, 2 * M], F32, name="angle_w", align_bytes=64)
+        table = keep.tile([P, 2 * M], F32, name="table", align_bytes=64)
+        nc.vector.tensor_copy(out=turns_i[:], in_=turns[:])
+        nc.vector.tensor_copy(out=turns_f[:], in_=turns_i[:])
+        nc.vector.tensor_sub(out=angle[:, 0:M], in0=turns[:], in1=turns_f[:])
+        nc.vector.tensor_scalar(out=angle[:, M : 2 * M], in0=angle[:, 0:M], scalar1=0.25, scalar2=None, op0=ALU.add)
+        nc.vector.scalar_tensor_tensor(
+            out=angle_w[:], in0=angle[:], scalar=0.5, in1=angle[:], op0=ALU.is_gt, op1=ALU.subtract
+        )
+        nc.scalar.activation(out=table[:], in_=angle_w[:], func=ACT.Sin, scale=-2.0 * math.pi)
+
+        xw = keep.tile([P, HID], BF16, name="xw", align_bytes=64)
+        nc.vector.tensor_copy(out=xw[:, 0:1024], in_=xb[:, 0:1024].bitcast(FP8))
+        nc.vector.tensor_copy(out=xw[:, 1024:2048], in_=xb[:, 1024:2048].bitcast(FP8))
+        x_codes = keep.tile([P, GROUPS * P], U32, name="x_codes", align_bytes=64)
+        x_planes = keep.tile([P, GROUPS * P], U8, name="x_planes", align_bytes=64)
+        x_words = xw[:].bitcast(F32)
+        gx = keep.tile([P, GROUPS * 512], BF16, name="gx", align_bytes=64)
+        x_trs = []
+        for pair in range(2):
+            xt = tr_pool.tile([P, 4, P], F32, name="tr", tag="tr")
+            for i in range(4):
+                g, u = 2 * pair + i // 2, i % 2
+                nc.tensor.transpose(xt[:, i, :], x_words[:, 256 * g + u : 256 * (g + 1) : 2], ident[:])
+            x_trs.append(xt)
+        for g in range(GROUPS):
+            src = x_trs[g // 2][:].bitcast(BF16)[:, 2 * (g % 2) : 2 * (g % 2) + 2, :]
+            nc.vector.tensor_tensor(
+                out=gx[:, 512 * g : 512 * (g + 1)].rearrange("p (n u e) -> p n u e", u=2, e=2),
+                in0=src.rearrange("p u (n e) -> p n u e", e=2),
+                in1=xs[:, g, :].rearrange("p (u e) -> p u e", e=2).unsqueeze(1).to_broadcast([P, P, 2, 2]),
+                op=ALU.mult,
+            )
+        for pair in range(2):
+            nc.vector.quantize_mx(
+                out=x_codes[:, 256 * pair : 256 * (pair + 1)].bitcast(FP8X4),
+                scales=x_planes[:, 256 * pair : 256 * (pair + 1)],
+                in_=gx[:, 1024 * pair : 1024 * (pair + 1)],
+            )
+
+        bias_sb = {}
+
+        def spread_bias(u):
+            c, half = u // 2, u % 2
+            z = c % 2
+            bc = bc_pool.tile([P, UNIT], BF16, name="bc", tag="bc")
+            for b in range(2):
+                block = ((c // 2) * HID + half * UNIT) // BANK + b
+                row = 4 * z + block // 3
+                off = (block % 3) * BANK
+                nc.tensor.matmul(
+                    bc[:, b * BANK : (b + 1) * BANK],
+                    lhsT=ident_b[:, row : row + 1].to_broadcast([P, P]),
+                    rhs=brow[:, off : off + BANK],
+                    start=True,
+                    stop=True,
+                )
+            sb = work.tile([P, UNIT], BF16, name="bias", tag="bias", bufs=3)
+            nc.scalar.copy(out=sb[:], in_=bc[:])
+            bias_sb[u] = sb
+
+        accs = {}
+
+        def mx_pass(acc, c, c0, g, col_in_acc, first, last):
+            z = c % 2
+            base = c0
+            while (c, base, g) not in loaded:
+                base -= BANK
+            w, k, width = loaded[(c, base, g)]
+            n = min(BANK, width)
+            col = (c // 2) * HID + c0
+            nc.tensor.matmul_mx(
+                out=acc[:, col_in_acc : col_in_acc + n],
+                lhsT=x_codes[:, P * g : P * (g + 1)].bitcast(FP8X4),
+                lhsT_scale=x_planes[:, P * g : P * (g + 1)],
+                rhs=w[:, k, c0 - base : c0 - base + n].bitcast(FP8X4),
+                rhs_scale=packed[z][4 * g : P, col : col + n],
+                start=first,
+                stop=last,
+            )
+
+        def project_bank(c, c0):
+            acc = acc_pool.tile([P, BANK], F32, name="acc", tag="acc")
+            accs[(2 * c + c0 // UNIT, (c0 % UNIT) // BANK)] = acc
+            for g in range(GROUPS):
+                mx_pass(acc, c, c0, g, 0, g == 0, g == GROUPS - 1)
+
+        xts, pts, rts, yts, trs, grouped, codes, planes = {}, {}, {}, {}, {}, {}, {}, {}
+
+        def open_unit(u):
+            xts[u] = work.tile([P, HG, 2 * M, 2], F32, name="xt", tag="xt", bufs=2)
+            pts[u] = work.tile([P, HG, M, 4], F32, name="pt", tag="pt", bufs=2)
+            rts[u] = work.tile([P, HG, M, 4], F32, name="rt", tag="rt", bufs=2)
+
+        def add_bias(u, b, lo=0, hi=4):
+            acc = accs[(u, b)]
+            nc.vector.tensor_tensor(
+                out=xts[u][:, 4 * b + lo : 4 * b + hi, :, :],
+                in0=acc[:, P * lo : P * hi].rearrange("p (a h k) -> p a k h", h=2, k=2 * M),
+                in1=bias_sb[u][:, BANK * b + P * lo : BANK * b + P * hi].rearrange("p (a h k) -> p a k h", h=2, k=2 * M),
+                op=ALU.add,
+            )
+
+        def x4(u):
+            return xts[u][:].rearrange("p a (m j) h -> p a m (j h)", j=2)
+
+        def products_vec(u, dst, trig, a0, a1, m0, m1):
+            if m1 > m0:
+                nc.vector.tensor_tensor(
+                    out=dst[:, a0:a1, m0:m1, :],
+                    in0=x4(u)[:, a0:a1, m0:m1, :],
+                    in1=table[:, trig * M + m0 : trig * M + m1].unsqueeze(1).unsqueeze(3).to_broadcast([P, a1 - a0, m1 - m0, 4]),
+                    op=ALU.mult,
+                )
+
+        def products_act(u, dst, trig, m0, m1, a0=0, a1=HG):
+            for m in range(m0, m1):
+                nc.scalar.activation(
+                    out=dst[:, a0:a1, m, :], in_=x4(u)[:, a0:a1, m, :], func=ACT.Copy, scale=table[:, trig * M + m : trig * M + m + 1]
+                )
+
+        def rotate(u, a0=0, a1=HG):
+            if u not in yts:
+                yts[u] = work.tile([P, 2, HG * M * 2], BF16, name="y", tag="y", bufs=2, align_bytes=64)
+            for half in range(2):
+                pv = pts[u][:, a0:a1].rearrange("p a (q m) (j h) -> p j (a q) h m", m=4, j=2)
+                rv = rts[u][:, a0:a1].rearrange("p a (q m) (j h) -> p j (a q) h m", m=4, j=2)
+                nc.vector.tensor_tensor(
+                    out=yts[u][:, half, 64 * a0 : 64 * a1].rearrange("p (a h m) -> p a h m", h=2, m=4),
+                    in0=pv[:, half],
+                    in1=rv[:, 1 - half],
+                    op=ALU.subtract if half == 0 else ALU.add,
+                )
+
+        def turn(u):
+            tr = tr_pool.tile([P, 4, P], F32, name="tr", tag="tr")
+            yw = yts[u][:].rearrange("p a k -> p (a k)").bitcast(F32)
+            for i in range(4):
+                nc.tensor.transpose(tr[:, i, :], yw[:, i:512:4], ident[:])
+            trs[u] = tr
+
+        def gather(u):
+            gr = work.tile([P, 1024], BF16, name="gr", tag="gr", bufs=2, align_bytes=64)
+            nc.scalar.copy(
+                out=gr[:].bitcast(F32).rearrange("p (h n w) -> p h n w", h=2, w=2),
+                in_=trs[u][:].rearrange("p (h w) n -> p h n w", w=2),
+            )
+            grouped[u] = gr
+
+        def quantize(u):
+            cd = work.tile([P, 256], U32, name="cd", tag="cd", bufs=6, align_bytes=64)
+            pl = work.tile([P, 256], U8, name="pl", tag="pl", bufs=6, align_bytes=64)
+            nc.vector.quantize_mx(out=cd[:].bitcast(FP8X4), scales=pl[:], in_=grouped[u][:])
+            codes[u], planes[u] = cd, pl
+
+        score = sc_pool.tile([P, TAGS * P], F32, name="score", tag="score")
+
+        def add_score(u):
+            c, half = u // 2, u % 2
+            if c % 2 == 0:
+                return
+            tag, uq = c // 2, u - 2
+            for h in range(2):
+                cols = slice(P * h, P * (h + 1))
+                nc.tensor.matmul_mx(
+                    out=score[:, P * tag : P * (tag + 1)],
+                    lhsT=codes[uq][:, cols].bitcast(FP8X4),
+                    lhsT_scale=planes[uq][:, cols],
+                    rhs=codes[u][:, cols].bitcast(FP8X4),
+                    rhs_scale=planes[u][:, cols],
+                    start=(half == 0 and h == 0),
+                    stop=(half == 1 and h == 1),
+                )
+
+        def project(u, b):
+            if u < UNITS:
+                c = u // 2
+                if b == 0:
+                    load_until(4 * c + AHEAD)
+                project_bank(c, (u % 2) * UNIT + b * BANK)
+
+        spread_bias(0)
+        spread_bias(1)
+        project(0, 0)
+        project(0, 1)
+        for u in range(UNITS - 1):
+            project(u + 1, 0)
+            if u + 2 < UNITS:
+                spread_bias(u + 2)
+            open_unit(u)
+            add_bias(u, 0)
+            add_bias(u, 1)
+            if u > 1:
+                quantize(u - 2)
+                add_score(u - 2)
+            if u:
+                rotate(u - 1)
+                turn(u - 1)
+            if u + 1 < UNITS - 1:
+                project(u + 1, 1)
+            products_act(u, rts[u], 0, 0, M)
+            products_act(u, pts[u], 1, VEC_M, M)
+            products_vec(u, pts[u], 1, 0, HG, 0, VEC_M)
+            if u:
+                gather(u - 1)
+
+        u = UNITS - 1
+        open_unit(u)
+        add_bias(u, 0)
+        quantize(u - 2)
+        add_score(u - 2)
+        rotate(u - 1)
+        turn(u - 1)
+        products_act(u, rts[u], 0, 0, M, 0, 4)
+        products_vec(u, pts[u], 1, 0, 4, 0, M)
+        gather(u - 1)
+        acc = acc_pool.tile([P, BANK], F32, name="acc", tag="acc")
+        accs[(u, 1)] = acc
+        for piece in range(2):
+            for g in range(GROUPS):
+                mx_pass(acc, 5, 1536 + 256 * piece, g, 256 * piece, g == 0, g == GROUPS - 1)
+        quantize(u - 1)
+        add_score(u - 1)
+        rotate(u, 0, 4)
+        for piece in range(2):
+            a0 = 4 + 2 * piece
+            add_bias(u, 1, 2 * piece, 2 * piece + 2)
+            products_vec(u, pts[u], 1, a0, a0 + 2, 0, M)
+            products_vec(u, rts[u], 0, a0, a0 + 2, 0, M)
+            rotate(u, a0, a0 + 2)
+        turn(u)
+        gather(u)
+        quantize(u)
+        add_score(u)
+
+        res = keep.tile([P, P * TAGS], F32, name="res", align_bytes=64)
+        nc.scalar.activation(
+            out=res[:].rearrange("p (j t) -> p j t", t=TAGS),
+            in_=score[:].rearrange("p (t j) -> p j t", t=TAGS),
+            func=ACT.Copy,
+            scale=SCORE_SCALE,
+        )
+        nc.sync.dma_start(out=out.rearrange("b i j t -> (b i) (j t)"), in_=res[:])

@@ -30,8 +30,9 @@ SCORE_SCALE = (HID // 12) ** (-0.5) / HEADS
 FLOPS = 2 * P * HID * 2 * NOUT + 2 * TAGS * P * P * HID
 
 VEC_M = 20
-W_BUFS = 18
-AHEAD = 14
+W_BUFS = 15
+AHEAD = 12
+SPREAD_HEAD = 6
 
 
 def tile_ner_w_w8_kernel(
@@ -45,9 +46,8 @@ def tile_ner_w_w8_kernel(
         keep = ctx.enter_context(tc.tile_pool(name="keep", bufs=1))
         wpool = ctx.enter_context(tc.tile_pool(name="weights", bufs=W_BUFS))
         work = ctx.enter_context(tc.tile_pool(name="work", bufs=2))
-        acc_pool = ctx.enter_context(tc.psum_pool(name="acc", bufs=4))
+        acc_pool = ctx.enter_context(tc.psum_pool(name="acc", bufs=5))
         tr_pool = ctx.enter_context(tc.psum_pool(name="tr", bufs=2))
-        bc_pool = ctx.enter_context(tc.psum_pool(name="bc", bufs=1))
         sc_pool = ctx.enter_context(tc.psum_pool(name="sc", bufs=1))
         ctx.enter_context(tc.manual_schedule())
 
@@ -73,11 +73,12 @@ def tile_ner_w_w8_kernel(
         nc.sync.dma_start(out=brow[0:4, :], in_=bq.rearrange("(r n) -> r n", r=4))
         nc.sync.dma_start(out=brow[4:8, :], in_=bk.rearrange("(r n) -> r n", r=4))
 
-        def load_scales(z):
+        def load_scales(c):
+            cols = slice((c // 2) * HID, (c // 2 + 1) * HID)
             for quad in range(4):
                 nc.sync.dma_start(
-                    out=packed[z][32 * quad : 32 * quad + 16, :].bitcast(I32),
-                    in_=wscales[z][:, 4 * quad : 4 * quad + 4, :].bitcast(I32),
+                    out=packed[c % 2][32 * quad : 32 * quad + 16, cols].bitcast(I32),
+                    in_=wscales[c % 2][:, 4 * quad : 4 * quad + 4, cols].bitcast(I32),
                 )
 
         plan = []
@@ -87,14 +88,11 @@ def tile_ner_w_w8_kernel(
         for c in range(1, 4):
             for g in range(GROUPS):
                 plan.append((c, 0, 2048, g, 1))
-        for c in (4, 5):
-            for half in range(2):
-                if c == 5 and half == 1:
-                    break
-                for g in (0, 2):
-                    plan.append((c, 1024 * half, 1024, g, 2))
-        plan.append((5, 1024, 512, 0, 2))
-        plan.append((5, 1024, 512, 2, 2))
+        for half in range(2):
+            for g in (0, 2):
+                plan.append((4, 1024 * half, 1024, g, 2))
+        for c0 in (0, 512, 1024):
+            plan.append((5, c0, 512, 0, 4))
         plan.append((5, 1536, 256, 0, 4))
         plan.append((5, 1792, 256, 0, 4))
         loaded = {}
@@ -103,10 +101,8 @@ def tile_ner_w_w8_kernel(
         def load_until(n):
             while count[0] < min(n, len(plan)):
                 c, c0, width, g, ng = plan[count[0]]
-                if count[0] == 0:
-                    load_scales(0)
-                if count[0] == 4:
-                    load_scales(1)
+                if c0 == 0 and g == 0:
+                    load_scales(c)
                 z = c % 2
                 col = (c // 2) * HID + c0
                 w = wpool.tile([P, ng, width], U32, name="w", tag="w", align_bytes=64)
@@ -170,12 +166,12 @@ def tile_ner_w_w8_kernel(
                 in_=gx[:, 1024 * pair : 1024 * (pair + 1)],
             )
 
-        bias_sb = {}
+        bias_all = keep.tile([P, UNITS * UNIT], BF16, name="bias_all", align_bytes=64)
 
         def spread_bias(u):
             c, half = u // 2, u % 2
             z = c % 2
-            bc = bc_pool.tile([P, UNIT], BF16, name="bc", tag="bc")
+            bc = acc_pool.tile([P, UNIT], BF16, name="bc", tag="acc")
             for b in range(2):
                 block = ((c // 2) * HID + half * UNIT) // BANK + b
                 row = 4 * z + block // 3
@@ -187,9 +183,7 @@ def tile_ner_w_w8_kernel(
                     start=True,
                     stop=True,
                 )
-            sb = work.tile([P, UNIT], BF16, name="bias", tag="bias", bufs=3)
-            nc.scalar.copy(out=sb[:], in_=bc[:])
-            bias_sb[u] = sb
+            nc.scalar.copy(out=bias_all[:, UNIT * u : UNIT * (u + 1)], in_=bc[:])
 
         accs = {}
 
@@ -229,7 +223,7 @@ def tile_ner_w_w8_kernel(
             nc.vector.tensor_tensor(
                 out=xts[u][:, 4 * b + lo : 4 * b + hi, :, :],
                 in0=acc[:, P * lo : P * hi].rearrange("p (a h k) -> p a k h", h=2, k=2 * M),
-                in1=bias_sb[u][:, BANK * b + P * lo : BANK * b + P * hi].rearrange("p (a h k) -> p a k h", h=2, k=2 * M),
+                in1=bias_all[:, UNIT * u + BANK * b + P * lo : UNIT * u + BANK * b + P * hi].rearrange("p (a h k) -> p a k h", h=2, k=2 * M),
                 op=ALU.add,
             )
 
@@ -253,22 +247,24 @@ def tile_ner_w_w8_kernel(
 
         def rotate(u, a0=0, a1=HG):
             if u not in yts:
-                yts[u] = work.tile([P, 2, HG * M * 2], BF16, name="y", tag="y", bufs=2, align_bytes=64)
+                yts[u] = work.tile([P, 4, 2, 2 * HG * 8], BF16, name="y", tag="y", bufs=2, align_bytes=64)
+            pv = pts[u][:, a0:a1].rearrange("p a (q w e) (j h) -> p w j (a q) e h", w=2, e=2, j=2)
+            rv = rts[u][:, a0:a1].rearrange("p a (q w e) (j h) -> p w j (a q) e h", w=2, e=2, j=2)
+            yv = yts[u][:].rearrange("p (h w) f (s e) -> p w f s e h", h=2, e=2)
             for half in range(2):
-                pv = pts[u][:, a0:a1].rearrange("p a (q m) (j h) -> p j (a q) h m", m=4, j=2)
-                rv = rts[u][:, a0:a1].rearrange("p a (q m) (j h) -> p j (a q) h m", m=4, j=2)
-                nc.vector.tensor_tensor(
-                    out=yts[u][:, half, 64 * a0 : 64 * a1].rearrange("p (a h m) -> p a h m", h=2, m=4),
-                    in0=pv[:, half],
-                    in1=rv[:, 1 - half],
-                    op=ALU.subtract if half == 0 else ALU.add,
-                )
+                for w in range(2):
+                    nc.vector.tensor_tensor(
+                        out=yv[:, w, half, 8 * a0 : 8 * a1],
+                        in0=pv[:, w, half],
+                        in1=rv[:, w, 1 - half],
+                        op=ALU.subtract if half == 0 else ALU.add,
+                    )
 
         def turn(u):
             tr = tr_pool.tile([P, 4, P], F32, name="tr", tag="tr")
-            yw = yts[u][:].rearrange("p a k -> p (a k)").bitcast(F32)
+            yw = yts[u][:].rearrange("p i f k -> p i (f k)").bitcast(F32)
             for i in range(4):
-                nc.tensor.transpose(tr[:, i, :], yw[:, i:512:4], ident[:])
+                nc.tensor.transpose(tr[:, i, :], yw[:, i, :], ident[:])
             trs[u] = tr
 
         def gather(u):
@@ -304,6 +300,32 @@ def tile_ner_w_w8_kernel(
                     stop=(half == 1 and h == 1),
                 )
 
+        def finish_unit(u):
+            gr = work.tile([P, 2, P, 4], BF16, name="gr", tag="gr", bufs=2, align_bytes=64)
+            cd = work.tile([P, 256], U32, name="cd", tag="cd", bufs=6, align_bytes=64)
+            pl = work.tile([P, 256], U8, name="pl", tag="pl", bufs=6, align_bytes=64)
+            codes[u], planes[u] = cd, pl
+            yw = yts[u][:].rearrange("p i f k -> p i (f k)").bitcast(F32)
+            halves = []
+            for h in range(2):
+                tr = tr_pool.tile([P, 2, P], F32, name="tr", tag="tr")
+                for w in range(2):
+                    nc.tensor.transpose(tr[:, w, :], yw[:, 2 * h + w, :], ident[:])
+                halves.append(tr)
+            for h in range(2):
+                copy = nc.scalar.copy if h == 0 else nc.vector.tensor_copy
+                copy(
+                    out=gr[:, h].rearrange("p n t -> p (n t)").bitcast(F32).rearrange("p (n w) -> p n w", w=2),
+                    in_=halves[h][:].rearrange("p w n -> p n w"),
+                )
+            for h in range(2):
+                nc.vector.quantize_mx(
+                    out=cd[:, P * h : P * (h + 1)].bitcast(FP8X4),
+                    scales=pl[:, P * h : P * (h + 1)],
+                    in_=gr[:, h].rearrange("p n t -> p (n t)"),
+                )
+            add_score(u)
+
         def project(u, b):
             if u < UNITS:
                 c = u // 2
@@ -311,59 +333,70 @@ def tile_ner_w_w8_kernel(
                     load_until(4 * c + AHEAD)
                 project_bank(c, (u % 2) * UNIT + b * BANK)
 
-        spread_bias(0)
-        spread_bias(1)
+        for u in range(SPREAD_HEAD):
+            spread_bias(u)
         project(0, 0)
         project(0, 1)
-        for u in range(UNITS - 1):
+        for u in range(10):
             project(u + 1, 0)
-            if u + 2 < UNITS:
-                spread_bias(u + 2)
             open_unit(u)
             add_bias(u, 0)
             add_bias(u, 1)
-            if u > 1:
-                quantize(u - 2)
-                add_score(u - 2)
             if u:
                 rotate(u - 1)
                 turn(u - 1)
-            if u + 1 < UNITS - 1:
+            if u < 9:
                 project(u + 1, 1)
+            if u > 1:
+                quantize(u - 2)
+                add_score(u - 2)
             products_act(u, rts[u], 0, 0, M)
             products_act(u, pts[u], 1, VEC_M, M)
             products_vec(u, pts[u], 1, 0, HG, 0, VEC_M)
             if u:
                 gather(u - 1)
+            if u + SPREAD_HEAD < UNITS:
+                spread_bias(u + SPREAD_HEAD)
 
-        u = UNITS - 1
-        open_unit(u)
-        add_bias(u, 0)
-        quantize(u - 2)
-        add_score(u - 2)
-        rotate(u - 1)
-        turn(u - 1)
-        products_act(u, rts[u], 0, 0, M, 0, 4)
-        products_vec(u, pts[u], 1, 0, 4, 0, M)
-        gather(u - 1)
+        open_unit(10)
+        project(10, 1)
+        add_bias(10, 0)
+        products_vec(10, pts[10], 1, 0, 4, 0, M)
+        products_act(10, rts[10], 0, 0, M, 0, 4)
+        rotate(9)
+        turn(9)
+        project(11, 0)
+        quantize(8)
+        add_bias(10, 1)
+        gather(9)
+        products_act(10, rts[10], 0, 0, M, 4, 8)
+        products_vec(10, pts[10], 1, 4, 8, 0, M)
+        rotate(10, 0, 4)
+        open_unit(11)
         acc = acc_pool.tile([P, BANK], F32, name="acc", tag="acc")
-        accs[(u, 1)] = acc
-        for piece in range(2):
-            for g in range(GROUPS):
-                mx_pass(acc, 5, 1536 + 256 * piece, g, 256 * piece, g == 0, g == GROUPS - 1)
-        quantize(u - 1)
-        add_score(u - 1)
-        rotate(u, 0, 4)
-        for piece in range(2):
-            a0 = 4 + 2 * piece
-            add_bias(u, 1, 2 * piece, 2 * piece + 2)
-            products_vec(u, pts[u], 1, a0, a0 + 2, 0, M)
-            products_vec(u, rts[u], 0, a0, a0 + 2, 0, M)
-            rotate(u, a0, a0 + 2)
-        turn(u)
-        gather(u)
-        quantize(u)
-        add_score(u)
+        accs[(11, 1)] = acc
+        for g in range(GROUPS):
+            mx_pass(acc, 5, 1536, g, 0, g == 0, g == GROUPS - 1)
+        add_bias(11, 0)
+        quantize(9)
+        products_act(11, rts[11], 0, 0, M, 0, 4)
+        products_vec(11, pts[11], 1, 0, 4, 0, M)
+        for g in range(GROUPS):
+            mx_pass(acc, 5, 1792, g, 256, g == 0, g == GROUPS - 1)
+        rotate(10, 4, 8)
+        turn(10)
+        gather(10)
+        add_bias(11, 1, 0, 2)
+        products_vec(11, pts[11], 1, 4, 6, 0, M)
+        products_vec(11, rts[11], 0, 4, 6, 0, M)
+        add_bias(11, 1, 2, 4)
+        rotate(11, 0, 4)
+        products_vec(11, pts[11], 1, 6, 8, 0, M)
+        products_vec(11, rts[11], 0, 6, 8, 0, M)
+        quantize(10)
+        add_score(10)
+        rotate(11, 4, 8)
+        finish_unit(11)
 
         res = keep.tile([P, P * TAGS], F32, name="res", align_bytes=64)
         nc.scalar.activation(

@@ -29,10 +29,11 @@ HG = 8
 SCORE_SCALE = (HID // 12) ** (-0.5) / HEADS
 FLOPS = 2 * P * HID * 2 * NOUT + 2 * TAGS * P * P * HID
 
-VEC_M = 20
+VEC_M = 26
 W_BUFS = 15
 AHEAD = 12
-SPREAD_HEAD = 6
+SPREAD_HEAD = 8
+ACT_B = 24
 
 
 def tile_ner_w_w8_kernel(
@@ -70,8 +71,6 @@ def tile_ner_w_w8_kernel(
 
         nc.sync.dma_start(out=xb[:], in_=x_bytes.rearrange("b l h -> (b l) h"))
         nc.sync.dma_start(out=xs[:], in_=x_scale.rearrange("a b (g p t) -> p (a b g) t", p=P, t=4))
-        nc.sync.dma_start(out=brow[0:4, :], in_=bq.rearrange("(r n) -> r n", r=4))
-        nc.sync.dma_start(out=brow[4:8, :], in_=bk.rearrange("(r n) -> r n", r=4))
 
         def load_scales(c):
             cols = slice((c // 2) * HID, (c // 2 + 1) * HID)
@@ -86,8 +85,13 @@ def tile_ner_w_w8_kernel(
             for g in (0, 2):
                 plan.append((0, 1024 * half, 1024, g, 2))
         for c in range(1, 4):
-            for g in range(GROUPS):
-                plan.append((c, 0, 2048, g, 1))
+            if c in (3,):
+                for half in range(2):
+                    for g in (0, 2):
+                        plan.append((c, 1024 * half, 1024, g, 2))
+            else:
+                for g in range(GROUPS):
+                    plan.append((c, 0, 2048, g, 1))
         for half in range(2):
             for g in (0, 2):
                 plan.append((4, 1024 * half, 1024, g, 2))
@@ -114,6 +118,9 @@ def tile_ner_w_w8_kernel(
                     loaded[(c, c0, g + k)] = (w, k, width)
                 count[0] += 1
 
+        load_until(1)
+        nc.sync.dma_start(out=brow[0:4, :], in_=bq.rearrange("(r n) -> r n", r=4))
+        nc.sync.dma_start(out=brow[4:8, :], in_=bk.rearrange("(r n) -> r n", r=4))
         load_until(AHEAD)
 
         turns = keep.tile([P, M], F32, name="turns", align_bytes=64)
@@ -205,11 +212,12 @@ def tile_ner_w_w8_kernel(
                 stop=last,
             )
 
-        def project_bank(c, c0):
-            acc = acc_pool.tile([P, BANK], F32, name="acc", tag="acc")
-            accs[(2 * c + c0 // UNIT, (c0 % UNIT) // BANK)] = acc
-            for g in range(GROUPS):
-                mx_pass(acc, c, c0, g, 0, g == 0, g == GROUPS - 1)
+        def open_bank(u, b):
+            accs[(u, b)] = acc_pool.tile([P, BANK], F32, name="acc", tag="acc")
+
+        def project_bank(u, b, groups):
+            for g in groups:
+                mx_pass(accs[(u, b)], u // 2, (u % 2) * UNIT + b * BANK, g, 0, g == 0, g == GROUPS - 1)
 
         xts, pts, rts, yts, trs, grouped, codes, planes = {}, {}, {}, {}, {}, {}, {}, {}
 
@@ -312,6 +320,7 @@ def tile_ner_w_w8_kernel(
                 for w in range(2):
                     nc.tensor.transpose(tr[:, w, :], yw[:, 2 * h + w, :], ident[:])
                 halves.append(tr)
+            add_score(u - 1)
             for h in range(2):
                 copy = nc.scalar.copy if h == 0 else nc.vector.tensor_copy
                 copy(
@@ -327,11 +336,16 @@ def tile_ner_w_w8_kernel(
             add_score(u)
 
         def project(u, b):
-            if u < UNITS:
-                c = u // 2
-                if b == 0:
-                    load_until(4 * c + AHEAD)
-                project_bank(c, (u % 2) * UNIT + b * BANK)
+            if b == 0:
+                load_until(4 * (u // 2) + AHEAD)
+            if u in (0, 1, 6, 7, 8, 9,):
+                for bank in range(2):
+                    if b == 0:
+                        open_bank(u, bank)
+                    project_bank(u, bank, (2 * b, 2 * b + 1))
+            else:
+                open_bank(u, b)
+                project_bank(u, b, range(GROUPS))
 
         for u in range(SPREAD_HEAD):
             spread_bias(u)
@@ -344,9 +358,10 @@ def tile_ner_w_w8_kernel(
             add_bias(u, 1)
             if u:
                 rotate(u - 1)
-                turn(u - 1)
             if u < 9:
                 project(u + 1, 1)
+            if u:
+                turn(u - 1)
             if u > 1:
                 quantize(u - 2)
                 add_score(u - 2)
@@ -361,41 +376,39 @@ def tile_ner_w_w8_kernel(
         open_unit(10)
         project(10, 1)
         add_bias(10, 0)
-        products_vec(10, pts[10], 1, 0, 4, 0, M)
-        products_act(10, rts[10], 0, 0, M, 0, 4)
         rotate(9)
         turn(9)
         project(11, 0)
         quantize(8)
         add_bias(10, 1)
         gather(9)
-        products_act(10, rts[10], 0, 0, M, 4, 8)
-        products_vec(10, pts[10], 1, 4, 8, 0, M)
-        rotate(10, 0, 4)
+        products_act(10, rts[10], 0, 0, M)
+        products_vec(10, pts[10], 1, 0, 8, 0, M)
         open_unit(11)
         acc = acc_pool.tile([P, BANK], F32, name="acc", tag="acc")
         accs[(11, 1)] = acc
         for g in range(GROUPS):
             mx_pass(acc, 5, 1536, g, 0, g == 0, g == GROUPS - 1)
         add_bias(11, 0)
+        products_act(11, rts[11], 0, 0, 32, 0, 4)
         quantize(9)
-        products_act(11, rts[11], 0, 0, M, 0, 4)
         products_vec(11, pts[11], 1, 0, 4, 0, M)
         for g in range(GROUPS):
             mx_pass(acc, 5, 1792, g, 256, g == 0, g == GROUPS - 1)
-        rotate(10, 4, 8)
-        turn(10)
-        gather(10)
         add_bias(11, 1, 0, 2)
+        rotate(10)
+        turn(10)
+        products_act(11, rts[11], 0, 0, 12, 4, 6)
+        gather(10)
         products_vec(11, pts[11], 1, 4, 6, 0, M)
-        products_vec(11, rts[11], 0, 4, 6, 0, M)
+        products_vec(11, rts[11], 0, 4, 6, 12, M)
+        products_vec(11, rts[11], 0, 0, 4, 32, M)
         add_bias(11, 1, 2, 4)
         rotate(11, 0, 4)
         products_vec(11, pts[11], 1, 6, 8, 0, M)
         products_vec(11, rts[11], 0, 6, 8, 0, M)
-        quantize(10)
-        add_score(10)
         rotate(11, 4, 8)
+        quantize(10)
         finish_unit(11)
 
         res = keep.tile([P, P * TAGS], F32, name="res", align_bytes=64)

import math
from contextlib import ExitStack

import concourse.mybir as mybir
from concourse.masks import make_identity

F32 = mybir.dt.float32
BF16 = mybir.dt.bfloat16
U32 = mybir.dt.uint32
I32 = mybir.dt.int32
U8 = mybir.dt.uint8
FP8 = mybir.dt.float8_e4m3fn
FP8X4 = mybir.dt.float8_e4m3fn_x4
ALU = mybir.AluOpType
ACT = mybir.ActivationFunctionType

P = 128
HID = 2048
TAGS = 3
HEADS = 32
DH = 64
M = DH // 2
GROUPS = HID // 512
NOUT = HID * TAGS
BANK = 512
UNIT = 1024
UNITS = 2 * NOUT // UNIT
HG = 8
SCORE_SCALE = (HID // 12) ** (-0.5) / HEADS
FLOPS = 2 * P * HID * 2 * NOUT + 2 * TAGS * P * P * HID

VEC_M = 26
W_BUFS = 15
AHEAD = 12
SPREAD_HEAD = 8
ACT_B = 24


def tile_ner_w_w8_kernel(
    tc, x_bytes, x_scale, wq_words, wq_scales, bq, wk_words, wk_scales, bk, out
):
    nc = tc.nc
    words = (wq_words, wk_words)
    wscales = (wq_scales, wk_scales)

    with ExitStack() as ctx:
        keep = ctx.enter_context(tc.tile_pool(name="keep", bufs=1))
        wpool = ctx.enter_context(tc.tile_pool(name="weights", bufs=W_BUFS))
        work = ctx.enter_context(tc.tile_pool(name="work", bufs=2))
        acc_pool = ctx.enter_context(tc.psum_pool(name="acc", bufs=5))
        tr_pool = ctx.enter_context(tc.psum_pool(name="tr", bufs=2))
        sc_pool = ctx.enter_context(tc.psum_pool(name="sc", bufs=1))
        ctx.enter_context(tc.manual_schedule())

        xb = keep.tile([P, HID], U8, name="xb", align_bytes=64)
        xs = keep.tile([P, GROUPS, 4], F32, name="xs", align_bytes=64)
        brow = keep.tile([P, 1536], BF16, name="brow", align_bytes=64)
        packed_q = keep.tile([P, NOUT], U8, name="packed_q", align_bytes=64)
        packed_k = keep.tile([P, NOUT], U8, name="packed_k", align_bytes=64)
        packed = (packed_q, packed_k)

        nc.gpsimd.memset(brow[:].bitcast(U32), 0)
        nc.vector.memset(packed_q[:].bitcast(I32), 0)
        pos = keep.tile([P, 1], F32, name="pos", align_bytes=64)
        nc.gpsimd.iota(pos[:], [[0, 1]], base=0, channel_multiplier=1, allow_small_or_imprecise_dtypes=True)
        ident = keep.tile([P, P], F32, name="ident", align_bytes=64)
        make_identity(nc, ident[:])
        ident_b = keep.tile([P, P], BF16, name="ident_b", align_bytes=64)
        make_identity(nc, ident_b[:])
        nc.gpsimd.memset(packed_k[:].bitcast(I32), 0)

        nc.sync.dma_start(out=xb[:], in_=x_bytes.rearrange("b l h -> (b l) h"))
        nc.sync.dma_start(out=xs[:], in_=x_scale.rearrange("a b (g p t) -> p (a b g) t", p=P, t=4))

        def load_scales(c):
            cols = slice((c // 2) * HID, (c // 2 + 1) * HID)
            for quad in range(4):
                nc.sync.dma_start(
                    out=packed[c % 2][32 * quad : 32 * quad + 16, cols].bitcast(I32),
                    in_=wscales[c % 2][:, 4 * quad : 4 * quad + 4, cols].bitcast(I32),
                )

        plan = []
        for half in range(2):
            for g in (0, 2):
                plan.append((0, 1024 * half, 1024, g, 2))
        for c in range(1, 4):
            if c in (3,):
                for half in range(2):
                    for g in (0, 2):
                        plan.append((c, 1024 * half, 1024, g, 2))
            else:
                for g in range(GROUPS):
                    plan.append((c, 0, 2048, g, 1))
        for half in range(2):
            for g in (0, 2):
                plan.append((4, 1024 * half, 1024, g, 2))
        for c0 in (0, 512, 1024):
            plan.append((5, c0, 512, 0, 4))
        plan.append((5, 1536, 256, 0, 4))
        plan.append((5, 1792, 256, 0, 4))
        loaded = {}
        count = [0]

        def load_until(n):
            while count[0] < min(n, len(plan)):
                c, c0, width, g, ng = plan[count[0]]
                if c0 == 0 and g == 0:
                    load_scales(c)
                z = c % 2
                col = (c // 2) * HID + c0
                w = wpool.tile([P, ng, width], U32, name="w", tag="w", align_bytes=64)
                nc.sync.dma_start(
                    out=w[:].bitcast(I32),
                    in_=words[z].rearrange("g p n t -> p g (n t)")[:, g : g + ng, 4 * col : 4 * (col + width)].bitcast(I32),
                )
                for k in range(ng):
                    loaded[(c, c0, g + k)] = (w, k, width)
                count[0] += 1

        load_until(1)
        nc.sync.dma_start(out=brow[0:4, :], in_=bq.rearrange("(r n) -> r n", r=4))
        nc.sync.dma_start(out=brow[4:8, :], in_=bk.rearrange("(r n) -> r n", r=4))
        load_until(AHEAD)

        turns = keep.tile([P, M], F32, name="turns", align_bytes=64)
        for m in range(8):
            nc.vector.tensor_scalar(
                out=turns[:, m : m + 1], in0=pos[:], scalar1=10000.0 ** (-m / M) / (2.0 * math.pi), scalar2=None, op0=ALU.mult
            )
        nc.vector.tensor_scalar(out=turns[:, 8:16], in0=turns[:, 0:8], scalar1=0.1, scalar2=None, op0=ALU.mult)
        nc.vector.tensor_scalar(out=turns[:, 16:32], in0=turns[:, 0:16], scalar1=0.01, scalar2=None, op0=ALU.mult)
        turns_i = keep.tile([P, M], I32, name="turns_i", align_bytes=64)
        turns_f = keep.tile([P, M], F32, name="turns_f", align_bytes=64)
        angle = keep.tile([P, 2 * M], F32, name="angle", align_bytes=64)
        angle_w = keep.tile([P, 2 * M], F32, name="angle_w", align_bytes=64)
        table = keep.tile([P, 2 * M], F32, name="table", align_bytes=64)
        nc.vector.tensor_copy(out=turns_i[:], in_=turns[:])
        nc.vector.tensor_copy(out=turns_f[:], in_=turns_i[:])
        nc.vector.tensor_sub(out=angle[:, 0:M], in0=turns[:], in1=turns_f[:])
        nc.vector.tensor_scalar(out=angle[:, M : 2 * M], in0=angle[:, 0:M], scalar1=0.25, scalar2=None, op0=ALU.add)
        nc.vector.scalar_tensor_tensor(
            out=angle_w[:], in0=angle[:], scalar=0.5, in1=angle[:], op0=ALU.is_gt, op1=ALU.subtract
        )
        nc.scalar.activation(out=table[:], in_=angle_w[:], func=ACT.Sin, scale=-2.0 * math.pi)

        xw = keep.tile([P, HID], BF16, name="xw", align_bytes=64)
        nc.vector.tensor_copy(out=xw[:, 0:1024], in_=xb[:, 0:1024].bitcast(FP8))
        nc.vector.tensor_copy(out=xw[:, 1024:2048], in_=xb[:, 1024:2048].bitcast(FP8))
        x_codes = keep.tile([P, GROUPS * P], U32, name="x_codes", align_bytes=64)
        x_planes = keep.tile([P, GROUPS * P], U8, name="x_planes", align_bytes=64)
        x_words = xw[:].bitcast(F32)
        gx = keep.tile([P, GROUPS * 512], BF16, name="gx", align_bytes=64)
        x_trs = []
        for pair in range(2):
            xt = tr_pool.tile([P, 4, P], F32, name="tr", tag="tr")
            for i in range(4):
                g, u = 2 * pair + i // 2, i % 2
                nc.tensor.transpose(xt[:, i, :], x_words[:, 256 * g + u : 256 * (g + 1) : 2], ident[:])
            x_trs.append(xt)
        for g in range(GROUPS):
            src = x_trs[g // 2][:].bitcast(BF16)[:, 2 * (g % 2) : 2 * (g % 2) + 2, :]
            nc.vector.tensor_tensor(
                out=gx[:, 512 * g : 512 * (g + 1)].rearrange("p (n u e) -> p n u e", u=2, e=2),
                in0=src.rearrange("p u (n e) -> p n u e", e=2),
                in1=xs[:, g, :].rearrange("p (u e) -> p u e", e=2).unsqueeze(1).to_broadcast([P, P, 2, 2]),
                op=ALU.mult,
            )
        for pair in range(2):
            nc.vector.quantize_mx(
                out=x_codes[:, 256 * pair : 256 * (pair + 1)].bitcast(FP8X4),
                scales=x_planes[:, 256 * pair : 256 * (pair + 1)],
                in_=gx[:, 1024 * pair : 1024 * (pair + 1)],
            )

        bias_all = keep.tile([P, UNITS * UNIT], BF16, name="bias_all", align_bytes=64)

        def spread_bias(u):
            c, half = u // 2, u % 2
            z = c % 2
            bc = acc_pool.tile([P, UNIT], BF16, name="bc", tag="acc")
            for b in range(2):
                block = ((c // 2) * HID + half * UNIT) // BANK + b
                row = 4 * z + block // 3
                off = (block % 3) * BANK
                nc.tensor.matmul(
                    bc[:, b * BANK : (b + 1) * BANK],
                    lhsT=ident_b[:, row : row + 1].to_broadcast([P, P]),
                    rhs=brow[:, off : off + BANK],
                    start=True,
                    stop=True,
                )
            nc.scalar.copy(out=bias_all[:, UNIT * u : UNIT * (u + 1)], in_=bc[:])

        accs = {}

        def mx_pass(acc, c, c0, g, col_in_acc, first, last):
            z = c % 2
            base = c0
            while (c, base, g) not in loaded:
                base -= BANK
            w, k, width = loaded[(c, base, g)]
            n = min(BANK, width)
            col = (c // 2) * HID + c0
            nc.tensor.matmul_mx(
                out=acc[:, col_in_acc : col_in_acc + n],
                lhsT=x_codes[:, P * g : P * (g + 1)].bitcast(FP8X4),
                lhsT_scale=x_planes[:, P * g : P * (g + 1)],
                rhs=w[:, k, c0 - base : c0 - base + n].bitcast(FP8X4),
                rhs_scale=packed[z][4 * g : P, col : col + n],
                start=first,
                stop=last,
            )

        def open_bank(u, b):
            accs[(u, b)] = acc_pool.tile([P, BANK], F32, name="acc", tag="acc")

        def project_bank(u, b, groups):
            for g in groups:
                mx_pass(accs[(u, b)], u // 2, (u % 2) * UNIT + b * BANK, g, 0, g == 0, g == GROUPS - 1)

        xts, pts, rts, yts, trs, grouped, codes, planes = {}, {}, {}, {}, {}, {}, {}, {}

        def open_unit(u):
            xts[u] = work.tile([P, HG, 2 * M, 2], F32, name="xt", tag="xt", bufs=2)
            pts[u] = work.tile([P, HG, M, 4], F32, name="pt", tag="pt", bufs=2)
            rts[u] = work.tile([P, HG, M, 4], F32, name="rt", tag="rt", bufs=2)

        def add_bias(u, b, lo=0, hi=4):
            acc = accs[(u, b)]
            nc.vector.tensor_tensor(
                out=xts[u][:, 4 * b + lo : 4 * b + hi, :, :],
                in0=acc[:, P * lo : P * hi].rearrange("p (a h k) -> p a k h", h=2, k=2 * M),
                in1=bias_all[:, UNIT * u + BANK * b + P * lo : UNIT * u + BANK * b + P * hi].rearrange("p (a h k) -> p a k h", h=2, k=2 * M),
                op=ALU.add,
            )

        def x4(u):
            return xts[u][:].rearrange("p a (m j) h -> p a m (j h)", j=2)

        def products_vec(u, dst, trig, a0, a1, m0, m1):
            if m1 > m0:
                nc.vector.tensor_tensor(
                    out=dst[:, a0:a1, m0:m1, :],
                    in0=x4(u)[:, a0:a1, m0:m1, :],
                    in1=table[:, trig * M + m0 : trig * M + m1].unsqueeze(1).unsqueeze(3).to_broadcast([P, a1 - a0, m1 - m0, 4]),
                    op=ALU.mult,
                )

        def products_act(u, dst, trig, m0, m1, a0=0, a1=HG):
            for m in range(m0, m1):
                nc.scalar.activation(
                    out=dst[:, a0:a1, m, :], in_=x4(u)[:, a0:a1, m, :], func=ACT.Copy, scale=table[:, trig * M + m : trig * M + m + 1]
                )

        def rotate(u, a0=0, a1=HG):
            if u not in yts:
                yts[u] = work.tile([P, 4, 2, 2 * HG * 8], BF16, name="y", tag="y", bufs=2, align_bytes=64)
            pv = pts[u][:, a0:a1].rearrange("p a (q w e) (j h) -> p w j (a q) e h", w=2, e=2, j=2)
            rv = rts[u][:, a0:a1].rearrange("p a (q w e) (j h) -> p w j (a q) e h", w=2, e=2, j=2)
            yv = yts[u][:].rearrange("p (h w) f (s e) -> p w f s e h", h=2, e=2)
            for half in range(2):
                for w in range(2):
                    nc.vector.tensor_tensor(
                        out=yv[:, w, half, 8 * a0 : 8 * a1],
                        in0=pv[:, w, half],
                        in1=rv[:, w, 1 - half],
                        op=ALU.subtract if half == 0 else ALU.add,
                    )

        def turn(u):
            tr = tr_pool.tile([P, 4, P], F32, name="tr", tag="tr")
            yw = yts[u][:].rearrange("p i f k -> p i (f k)").bitcast(F32)
            for i in range(4):
                nc.tensor.transpose(tr[:, i, :], yw[:, i, :], ident[:])
            trs[u] = tr

        def gather(u):
            gr = work.tile([P, 1024], BF16, name="gr", tag="gr", bufs=2, align_bytes=64)
            nc.scalar.copy(
                out=gr[:].bitcast(F32).rearrange("p (h n w) -> p h n w", h=2, w=2),
                in_=trs[u][:].rearrange("p (h w) n -> p h n w", w=2),
            )
            grouped[u] = gr

        def quantize(u):
            cd = work.tile([P, 256], U32, name="cd", tag="cd", bufs=6, align_bytes=64)
            pl = work.tile([P, 256], U8, name="pl", tag="pl", bufs=6, align_bytes=64)
            nc.vector.quantize_mx(out=cd[:].bitcast(FP8X4), scales=pl[:], in_=grouped[u][:])
            codes[u], planes[u] = cd, pl

        score = sc_pool.tile([P, TAGS * P], F32, name="score", tag="score")

        def add_score(u):
            c, half = u // 2, u % 2
            if c % 2 == 0:
                return
            tag, uq = c // 2, u - 2
            for h in range(2):
                cols = slice(P * h, P * (h + 1))
                nc.tensor.matmul_mx(
                    out=score[:, P * tag : P * (tag + 1)],
                    lhsT=codes[uq][:, cols].bitcast(FP8X4),
                    lhsT_scale=planes[uq][:, cols],
                    rhs=codes[u][:, cols].bitcast(FP8X4),
                    rhs_scale=planes[u][:, cols],
                    start=(half == 0 and h == 0),
                    stop=(half == 1 and h == 1),
                )

        def finish_unit(u):
            gr = work.tile([P, 2, P, 4], BF16, name="gr", tag="gr", bufs=2, align_bytes=64)
            cd = work.tile([P, 256], U32, name="cd", tag="cd", bufs=6, align_bytes=64)
            pl = work.tile([P, 256], U8, name="pl", tag="pl", bufs=6, align_bytes=64)
            codes[u], planes[u] = cd, pl
            yw = yts[u][:].rearrange("p i f k -> p i (f k)").bitcast(F32)
            halves = []
            for h in range(2):
                tr = tr_pool.tile([P, 2, P], F32, name="tr", tag="tr")
                for w in range(2):
                    nc.tensor.transpose(tr[:, w, :], yw[:, 2 * h + w, :], ident[:])
                halves.append(tr)
            add_score(u - 1)
            for h in range(2):
                copy = nc.scalar.copy if h == 0 else nc.vector.tensor_copy
                copy(
                    out=gr[:, h].rearrange("p n t -> p (n t)").bitcast(F32).rearrange("p (n w) -> p n w", w=2),
                    in_=halves[h][:].rearrange("p w n -> p n w"),
                )
            for h in range(2):
                nc.vector.quantize_mx(
                    out=cd[:, P * h : P * (h + 1)].bitcast(FP8X4),
                    scales=pl[:, P * h : P * (h + 1)],
                    in_=gr[:, h].rearrange("p n t -> p (n t)"),
                )
            add_score(u)

        def project(u, b):
            if b == 0:
                load_until(4 * (u // 2) + AHEAD)
            if u in (0, 1, 6, 7, 8, 9,):
                for bank in range(2):
                    if b == 0:
                        open_bank(u, bank)
                    project_bank(u, bank, (2 * b, 2 * b + 1))
            else:
                open_bank(u, b)
                project_bank(u, b, range(GROUPS))

        for u in range(SPREAD_HEAD):
            spread_bias(u)
        project(0, 0)
        project(0, 1)
        for u in range(10):
            project(u + 1, 0)
            open_unit(u)
            add_bias(u, 0)
            add_bias(u, 1)
            if u:
                rotate(u - 1)
            if u < 9:
                project(u + 1, 1)
            if u:
                turn(u - 1)
            if u > 1:
                quantize(u - 2)
                add_score(u - 2)
            products_act(u, rts[u], 0, 0, M)
            products_act(u, pts[u], 1, VEC_M, M)
            products_vec(u, pts[u], 1, 0, HG, 0, VEC_M)
            if u:
                gather(u - 1)
            if u + SPREAD_HEAD < UNITS:
                spread_bias(u + SPREAD_HEAD)

        open_unit(10)
        project(10, 1)
        add_bias(10, 0)
        rotate(9)
        turn(9)
        project(11, 0)
        quantize(8)
        add_bias(10, 1)
        gather(9)
        products_act(10, rts[10], 0, 0, M)
        products_vec(10, pts[10], 1, 0, 8, 0, M)
        open_unit(11)
        acc = acc_pool.tile([P, BANK], F32, name="acc", tag="acc")
        accs[(11, 1)] = acc
        for g in range(GROUPS):
            mx_pass(acc, 5, 1536, g, 0, g == 0, g == GROUPS - 1)
        add_bias(11, 0)
        products_act(11, rts[11], 0, 0, 32, 0, 4)
        quantize(9)
        products_vec(11, pts[11], 1, 0, 4, 0, M)
        for g in range(GROUPS):
            mx_pass(acc, 5, 1792, g, 256, g == 0, g == GROUPS - 1)
        add_bias(11, 1, 0, 2)
        rotate(10)
        turn(10)
        products_act(11, rts[11], 0, 0, 12, 4, 6)
        gather(10)
        products_vec(11, pts[11], 1, 4, 6, 0, M)
        products_vec(11, rts[11], 0, 4, 6, 12, M)
        products_vec(11, rts[11], 0, 0, 4, 32, M)
        add_bias(11, 1, 2, 4)
        rotate(11, 0, 4)
        products_vec(11, pts[11], 1, 6, 8, 0, M)
        products_vec(11, rts[11], 0, 6, 8, 0, M)
        rotate(11, 4, 8)
        quantize(10)
        finish_unit(11)

        res = keep.tile([P, P * TAGS], F32, name="res", align_bytes=64)
        nc.scalar.activation(
            out=res[:].rearrange("p (j t) -> p j t", t=TAGS),
            in_=score[:].rearrange("p (t j) -> p j t", t=TAGS),
            func=ACT.Copy,
            scale=SCORE_SCALE,
        )
        nc.sync.dma_start(out=out.rearrange("b i j t -> (b i) (j t)"), in_=res[:])
